import numpy as np
import ml_dtypes


def mxq(x, axis, fmt="e4m3"):
    dtype, down = {"e4m3": (ml_dtypes.float8_e4m3fn, 7), "e5m2": (ml_dtypes.float8_e5m2, 14)}[fmt]
    v = np.moveaxis(np.asarray(x, np.float32).astype(ml_dtypes.bfloat16).astype(np.float64), axis, -1)
    blocks = v.reshape(v.shape[:-1] + (-1, 32))
    amax = np.abs(blocks).max(-1, keepdims=True)
    byte = np.maximum(np.where(amax > 0, np.frexp(amax)[1] - 1 + 127, 0) - down, 1)
    scale = np.exp2(byte - 127.0)
    codes = (blocks / scale).astype(np.float32).astype(dtype).astype(np.float64)
    return np.moveaxis((codes * scale).reshape(v.shape), -1, axis)


WIDE = False


def mx_kscale(k):
    if not WIDE:
        return np.ones(k)
    levels = np.array([10, -10, 5, -5, 0])
    a = np.random.permutation(np.resize(levels, k // 512 * 4)).reshape(k // 512, 4)
    idx = np.arange(k)
    return np.exp2(a[idx // 512, idx % 128 // 32])


BF16 = ml_dtypes.bfloat16


def bf(x):
    return np.asarray(x, np.float32).astype(BF16)


def f64(x):
    return np.asarray(x).astype(np.float64)


E2M1 = np.array([0.0, 0.5, 1.0, 1.5, 2.0, 3.0, 4.0, 6.0, -0.0, -0.5, -1.0, -1.5, -2.0, -3.0, -4.0, -6.0])


def pack_weight(w, fmt):
    k, n = w.shape
    w = f64(bf(w)).reshape(k // 32, 32, n)
    amax = np.abs(w).max(1)
    if fmt == "e4m3":
        byte = np.frexp(amax)[1] - 1 + 127 - 7
    else:
        mant, ex = np.frexp(amax / 6.0)
        byte = np.where(mant > 0.5, ex, ex - 1) + 127
    byte = np.clip(np.where(amax > 0, byte, 1), 1, 254)
    scaled = (w * np.exp2(127.0 - byte)[:, None, :]).reshape(k, n).astype(np.float32)
    by_word = np.ascontiguousarray(scaled.reshape(k // 512, 128, 4, n).transpose(0, 1, 3, 2))
    if fmt == "e4m3":
        words = by_word.astype(ml_dtypes.float8_e4m3fn).view(np.uint8)
    else:
        c = by_word.astype(ml_dtypes.float4_e2m1fn).view(np.uint8) & 0xF
        words = c[..., 0::2] | (c[..., 1::2] << 4)
    return np.ascontiguousarray(words), np.ascontiguousarray(byte.astype(np.uint8).reshape(k // 512, 16, n))


def unpack_weight(words, scales, fmt):
    g, p, n, _ = words.shape
    if fmt == "e4m3":
        vals = np.ascontiguousarray(words).view(ml_dtypes.float8_e4m3fn).astype(np.float64)
    else:
        nib = np.empty((g, p, n, 4), np.uint8)
        nib[..., 0::2] = words & 0xF
        nib[..., 1::2] = words >> 4
        vals = E2M1[nib]
    vals = vals * np.repeat(np.exp2(scales.astype(np.float64) - 127.0), 8, axis=1)[..., None]
    return vals.transpose(0, 1, 3, 2).reshape(g * 512, n)

def pack4(w):
    words, scales = pack_weight(w, "e2m1")
    return words.reshape(words.shape[0], 128, -1), scales


def unpack4(words, scales):
    return unpack_weight(words.reshape(words.shape[0], 128, -1, 2), scales, "e2m1")


T, D, F, R = 512, 1024, 2560, 128


def setup_inputs():
    s = mx_kscale(F)
    h = bf(np.random.standard_normal((T, F)) * 0.75 * s)
    ha = bf(np.random.standard_normal((T, R)) * 0.75)
    words, scales = pack4(np.random.standard_normal((F, D)) / np.sqrt(F) / s[:, None])
    B_down = bf(np.random.standard_normal((R, D)) * 0.5 / np.sqrt(R))
    return {
        "h": h,
        "ha": ha,
        "W_down_words": words,
        "W_down_scales": scales,
        "B_down": B_down,
    }


def reference(h, ha, W_down_words, W_down_scales, B_down):
    return (mxq(f64(h), 1, "e4m3") @ unpack4(W_down_words, W_down_scales)) + f64(ha) @ f64(B_down)

@@ -1,0 +1,126 @@
+from contextlib import ExitStack
+
+import concourse.mybir as mybir
+from concourse.masks import make_identity
+
+F32 = mybir.dt.float32
+BF16 = mybir.dt.bfloat16
+I32 = mybir.dt.int32
+U32 = mybir.dt.uint32
+U8 = mybir.dt.uint8
+FP8X4 = mybir.dt.float8_e4m3fn_x4
+FP4X4 = mybir.dt.float4_e2m1fn_x4
+
+T, D, F, R = 512, 1024, 2560, 128
+P = 128
+PACK = 4
+K_PASS = P * PACK
+PASSES = F // K_PASS
+TOKEN_TILES = T // P
+N_COLS = 512
+N_HALVES = D // N_COLS
+WORDS = K_PASS // 2
+PASSES_PER_BANK = 2
+
+FLOPS = 2 * T * F * D + 2 * T * R * D
+
+
+def tile_loramlp_pb_kernel(tc, h, ha, W_down_words, W_down_scales, B_down, out):
+    nc = tc.nc
+    with ExitStack() as ctx:
+        keep = ctx.enter_context(tc.tile_pool(name="keep", bufs=1))
+        stage = ctx.enter_context(tc.tile_pool(name="stage", bufs=4))
+        flipped = ctx.enter_context(tc.psum_pool(name="flipped", bufs=4))
+        products = ctx.enter_context(tc.psum_pool(name="products", bufs=4))
+        ctx.enter_context(tc.manual_schedule())
+
+        h_sb = keep.tile([P, TOKEN_TILES, F], BF16)
+        ha_sb = keep.tile([P, TOKEN_TILES, R], BF16)
+        haT_sb = keep.tile([P, TOKEN_TILES, P], BF16)
+        b_sb = keep.tile([P, D], BF16)
+        w_words = keep.tile([P, PASSES, 2 * D], U8, align_bytes=64)
+        w_scales = keep.tile([P, PASSES, D], U8, align_bytes=64)
+        h_codes = keep.tile([P, TOKEN_TILES, PASSES, P], U32, align_bytes=64)
+        h_scales = keep.tile([P, TOKEN_TILES, PASSES, P], U8, align_bytes=64)
+        out_sb = keep.tile([P, TOKEN_TILES, D], F32)
+        ident_f32 = keep.tile([P, P], F32)
+        ident_bf16 = keep.tile([P, P], BF16)
+
+        nc.vector.memset(w_scales[:].bitcast(I32), 0)
+        make_identity(nc, ident_f32[:])
+        nc.vector.tensor_copy(out=ident_bf16[:], in_=ident_f32[:])
+
+        def load_h(m):
+            nc.sync.dma_start(out=h_sb[:, m, :], in_=h[m * P : (m + 1) * P, :])
+
+        nc.sync.dma_start(out=ha_sb[:], in_=ha.rearrange("(m p) r -> p m r", p=P))
+        nc.sync.dma_start(out=b_sb[:], in_=B_down)
+        load_h(0)
+        load_h(1)
+        for q in range(8):
+            row = 32 * (q // 4) + q % 4
+            nc.sync.dma_start(
+                out=w_scales[row : P : 64, :, :].bitcast(I32),
+                in_=W_down_scales[:, q : 16 : 8, :].rearrange("g q c -> q g c").bitcast(I32),
+            )
+        for g in range(PASSES):
+            nc.sync.dma_start(out=w_words[:, g, :].bitcast(I32), in_=W_down_words[g].bitcast(I32))
+        load_h(2)
+        load_h(3)
+
+        haT_ps = flipped.tile([P, TOKEN_TILES, P], BF16, tag="flipped")
+        for m in range(TOKEN_TILES):
+            nc.tensor.transpose(haT_ps[:, m, :], ha_sb[:, m, :], ident_bf16[:])
+        nc.scalar.copy(out=haT_sb[:], in_=haT_ps[:])
+        for m in range(TOKEN_TILES):
+            for n in range(N_HALVES):
+                cols = slice(n * N_COLS, (n + 1) * N_COLS)
+                lora = products.tile([P, N_COLS], F32, tag="product")
+                nc.tensor.matmul(lora[:], lhsT=haT_sb[:, m, :], rhs=b_sb[:, cols], start=True, stop=True)
+                if n == 0:
+                    nc.scalar.copy(out=out_sb[:, m, cols], in_=lora[:])
+                else:
+                    nc.vector.tensor_copy(out=out_sb[:, m, cols], in_=lora[:])
+
+        def quantise_tokens(m):
+            h_pairs = h_sb[:, m, :].bitcast(F32)
+            for g0 in range(0, PASSES, PASSES_PER_BANK):
+                count = min(PASSES_PER_BANK, PASSES - g0)
+                pairsT = flipped.tile([P, PASSES_PER_BANK, 2, P], F32, tag="flipped")
+                for c in range(count):
+                    words = h_pairs[:, (g0 + c) * WORDS : (g0 + c + 1) * WORDS]
+                    for u in range(2):
+                        nc.tensor.transpose(pairsT[:, c, u, :], words[:, u:WORDS:2], ident_f32[:])
+                grouped = stage.tile([P, PASSES_PER_BANK, P, PACK], BF16, align_bytes=64)
+                nc.scalar.copy(
+                    out=grouped[:, :count].bitcast(F32),
+                    in_=pairsT[:, :count].rearrange("p c u r -> p c r u"),
+                )
+                nc.vector.quantize_mx(
+                    out=h_codes[:, m, g0 : g0 + count, :].rearrange("p c r -> p (c r)").bitcast(FP8X4),
+                    scales=h_scales[:, m, g0 : g0 + count, :].rearrange("p c r -> p (c r)"),
+                    in_=grouped[:, :count].rearrange("p c r t -> p (c r t)"),
+                )
+
+        def multiply_tokens(m):
+            for n in range(N_HALVES):
+                cols = slice(n * N_COLS, (n + 1) * N_COLS)
+                acc = products.tile([P, N_COLS], F32, tag="product")
+                for g in range(PASSES):
+                    nc.tensor.matmul_mx(
+                        out=acc[:],
+                        lhsT=h_codes[:, m, g, :].bitcast(FP8X4),
+                        lhsT_scale=h_scales[:, m, g, :],
+                        rhs=w_words[:, g, 2 * n * N_COLS : 2 * (n + 1) * N_COLS].bitcast(FP4X4),
+                        rhs_scale=w_scales[:, g, cols],
+                        start=(g == 0),
+                        stop=(g == PASSES - 1),
+                    )
+                nc.vector.tensor_add(out=out_sb[:, m, cols], in0=acc[:], in1=out_sb[:, m, cols])
+                nc.sync.dma_start(out=out[m * P : (m + 1) * P, cols], in_=out_sb[:, m, cols])
+
+        quantise_tokens(0)
+        for m in range(TOKEN_TILES):
+            if m + 1 < TOKEN_TILES:
+                quantise_tokens(m + 1)
+            multiply_tokens(m)

@@ -19,8 +19,8 @@ PASSES = F // K_PASS
 TOKEN_TILES = T // P
 N_COLS = 512
 N_HALVES = D // N_COLS
-WORDS = K_PASS // 2
 PASSES_PER_BANK = 2
+AHEAD = 2
 
 FLOPS = 2 * T * F * D + 2 * T * R * D
 
@@ -35,6 +35,7 @@ def tile_loramlp_pb_kernel(tc, h, ha, W_down_words, W_down_scales, B_down, out):
         ctx.enter_context(tc.manual_schedule())
 
         h_sb = keep.tile([P, TOKEN_TILES, F], BF16)
+        h_sorted = keep.tile([P, TOKEN_TILES, 2, PASSES, P], F32)
         ha_sb = keep.tile([P, TOKEN_TILES, R], BF16)
         haT_sb = keep.tile([P, TOKEN_TILES, P], BF16)
         b_sb = keep.tile([P, D], BF16)
@@ -72,25 +73,27 @@ def tile_loramlp_pb_kernel(tc, h, ha, W_down_words, W_down_scales, B_down, out):
         for m in range(TOKEN_TILES):
             nc.tensor.transpose(haT_ps[:, m, :], ha_sb[:, m, :], ident_bf16[:])
         nc.scalar.copy(out=haT_sb[:], in_=haT_ps[:])
-        for m in range(TOKEN_TILES):
+
+        def sort_words(m):
+            nc.vector.tensor_copy(
+                out=h_sorted[:, m],
+                in_=h_sb[:, m, :].bitcast(F32).rearrange("r (g p u) -> r u g p", g=PASSES, u=2),
+            )
+
+        def lora_tokens(m):
             for n in range(N_HALVES):
                 cols = slice(n * N_COLS, (n + 1) * N_COLS)
                 lora = products.tile([P, N_COLS], F32, tag="product")
                 nc.tensor.matmul(lora[:], lhsT=haT_sb[:, m, :], rhs=b_sb[:, cols], start=True, stop=True)
-                if n == 0:
-                    nc.scalar.copy(out=out_sb[:, m, cols], in_=lora[:])
-                else:
-                    nc.vector.tensor_copy(out=out_sb[:, m, cols], in_=lora[:])
+                nc.scalar.copy(out=out_sb[:, m, cols], in_=lora[:])
 
         def quantise_tokens(m):
-            h_pairs = h_sb[:, m, :].bitcast(F32)
             for g0 in range(0, PASSES, PASSES_PER_BANK):
                 count = min(PASSES_PER_BANK, PASSES - g0)
                 pairsT = flipped.tile([P, PASSES_PER_BANK, 2, P], F32, tag="flipped")
                 for c in range(count):
-                    words = h_pairs[:, (g0 + c) * WORDS : (g0 + c + 1) * WORDS]
                     for u in range(2):
-                        nc.tensor.transpose(pairsT[:, c, u, :], words[:, u:WORDS:2], ident_f32[:])
+                        nc.tensor.transpose(pairsT[:, c, u, :], h_sorted[:, m, u, g0 + c, :], ident_f32[:])
                 grouped = stage.tile([P, PASSES_PER_BANK, P, PACK], BF16, align_bytes=64)
                 nc.scalar.copy(
                     out=grouped[:, :count].bitcast(F32),
@@ -119,8 +122,16 @@ def tile_loramlp_pb_kernel(tc, h, ha, W_down_words, W_down_scales, B_down, out):
                 nc.vector.tensor_add(out=out_sb[:, m, cols], in0=acc[:], in1=out_sb[:, m, cols])
                 nc.sync.dma_start(out=out[m * P : (m + 1) * P, cols], in_=out_sb[:, m, cols])
 
-        quantise_tokens(0)
+        for m in range(AHEAD):
+            sort_words(m)
+        for m in range(AHEAD):
+            lora_tokens(m)
+        for m in range(AHEAD):
+            quantise_tokens(m)
         for m in range(TOKEN_TILES):
-            if m + 1 < TOKEN_TILES:
-                quantise_tokens(m + 1)
+            if m + AHEAD < TOKEN_TILES:
+                sort_words(m + AHEAD)
             multiply_tokens(m)
+            if m + AHEAD < TOKEN_TILES:
+                lora_tokens(m + AHEAD)
+                quantise_tokens(m + AHEAD)

@@ -20,7 +20,8 @@ TOKEN_TILES = T // P
 N_COLS = 512
 N_HALVES = D // N_COLS
 PASSES_PER_BANK = 2
-AHEAD = 2
+TILES_PER_ROUND = 2
+STORE_COLS = 256
 
 FLOPS = 2 * T * F * D + 2 * T * R * D
 
@@ -29,7 +30,7 @@ def tile_loramlp_pb_kernel(tc, h, ha, W_down_words, W_down_scales, B_down, out):
     nc = tc.nc
     with ExitStack() as ctx:
         keep = ctx.enter_context(tc.tile_pool(name="keep", bufs=1))
-        stage = ctx.enter_context(tc.tile_pool(name="stage", bufs=4))
+        stage = ctx.enter_context(tc.tile_pool(name="stage", bufs=6))
         flipped = ctx.enter_context(tc.psum_pool(name="flipped", bufs=4))
         products = ctx.enter_context(tc.psum_pool(name="products", bufs=4))
         ctx.enter_context(tc.manual_schedule())
@@ -58,21 +59,25 @@ def tile_loramlp_pb_kernel(tc, h, ha, W_down_words, W_down_scales, B_down, out):
         nc.sync.dma_start(out=b_sb[:], in_=B_down)
         load_h(0)
         load_h(1)
-        for q in range(8):
-            row = 32 * (q // 4) + q % 4
+        for r in range(4):
             nc.sync.dma_start(
-                out=w_scales[row : P : 64, :, :].bitcast(I32),
-                in_=W_down_scales[:, q : 16 : 8, :].rearrange("g q c -> q g c").bitcast(I32),
+                out=w_scales[r : P : 32, :, :].bitcast(I32),
+                in_=W_down_scales[:, r : 16 : 4, :].rearrange("g q c -> q g c").bitcast(I32),
             )
-        for g in range(PASSES):
-            nc.sync.dma_start(out=w_words[:, g, :].bitcast(I32), in_=W_down_words[g].bitcast(I32))
+        for n in range(N_HALVES):
+            word_bytes = slice(2 * n * N_COLS, 2 * (n + 1) * N_COLS)
+            for g in range(PASSES):
+                nc.sync.dma_start(
+                    out=w_words[:, g, word_bytes].bitcast(I32),
+                    in_=W_down_words[g, :, word_bytes].bitcast(I32),
+                )
         load_h(2)
         load_h(3)
 
-        haT_ps = flipped.tile([P, TOKEN_TILES, P], BF16, tag="flipped")
         for m in range(TOKEN_TILES):
-            nc.tensor.transpose(haT_ps[:, m, :], ha_sb[:, m, :], ident_bf16[:])
-        nc.scalar.copy(out=haT_sb[:], in_=haT_ps[:])
+            haT_ps = flipped.tile([P, P], BF16, tag="flipped")
+            nc.tensor.transpose(haT_ps[:], ha_sb[:, m, :], ident_bf16[:])
+            nc.scalar.copy(out=haT_sb[:, m, :], in_=haT_ps[:])
 
         def sort_words(m):
             nc.vector.tensor_copy(
@@ -85,7 +90,10 @@ def tile_loramlp_pb_kernel(tc, h, ha, W_down_words, W_down_scales, B_down, out):
                 cols = slice(n * N_COLS, (n + 1) * N_COLS)
                 lora = products.tile([P, N_COLS], F32, tag="product")
                 nc.tensor.matmul(lora[:], lhsT=haT_sb[:, m, :], rhs=b_sb[:, cols], start=True, stop=True)
-                nc.scalar.copy(out=out_sb[:, m, cols], in_=lora[:])
+                if m % 2 == 1 and n == 1:
+                    nc.vector.tensor_copy(out=out_sb[:, m, cols], in_=lora[:])
+                else:
+                    nc.scalar.copy(out=out_sb[:, m, cols], in_=lora[:])
 
         def quantise_tokens(m):
             for g0 in range(0, PASSES, PASSES_PER_BANK):
@@ -119,19 +127,25 @@ def tile_loramlp_pb_kernel(tc, h, ha, W_down_words, W_down_scales, B_down, out):
                         start=(g == 0),
                         stop=(g == PASSES - 1),
                     )
-                nc.vector.tensor_add(out=out_sb[:, m, cols], in0=acc[:], in1=out_sb[:, m, cols])
-                nc.sync.dma_start(out=out[m * P : (m + 1) * P, cols], in_=out_sb[:, m, cols])
+                for first in range(0, N_COLS, STORE_COLS):
+                    part = slice(n * N_COLS + first, n * N_COLS + first + STORE_COLS)
+                    nc.vector.tensor_add(
+                        out=out_sb[:, m, part], in0=acc[:, first : first + STORE_COLS], in1=out_sb[:, m, part]
+                    )
+                    nc.sync.dma_start(out=out[m * P : (m + 1) * P, part], in_=out_sb[:, m, part])
 
-        for m in range(AHEAD):
-            sort_words(m)
-        for m in range(AHEAD):
-            lora_tokens(m)
-        for m in range(AHEAD):
-            quantise_tokens(m)
-        for m in range(TOKEN_TILES):
-            if m + AHEAD < TOKEN_TILES:
-                sort_words(m + AHEAD)
-            multiply_tokens(m)
-            if m + AHEAD < TOKEN_TILES:
-                lora_tokens(m + AHEAD)
-                quantise_tokens(m + AHEAD)
+        for i in range(TILES_PER_ROUND):
+            sort_words(i)
+            lora_tokens(2 * i)
+            lora_tokens(2 * i + 1)
+        for i in range(TILES_PER_ROUND):
+            quantise_tokens(i)
+
+        for m0 in range(0, TOKEN_TILES, TILES_PER_ROUND):
+            upcoming = range(m0 + TILES_PER_ROUND, min(m0 + 2 * TILES_PER_ROUND, TOKEN_TILES))
+            multiply_tokens(m0)
+            for m in upcoming:
+                sort_words(m)
+            multiply_tokens(m0 + 1)
+            for m in upcoming:
+                quantise_tokens(m)

@@ -85,15 +85,14 @@ def tile_loramlp_pb_kernel(tc, h, ha, W_down_words, W_down_scales, B_down, out):
                 in_=h_sb[:, m, :].bitcast(F32).rearrange("r (g p u) -> r u g p", g=PASSES, u=2),
             )
 
-        def lora_tokens(m):
-            for n in range(N_HALVES):
-                cols = slice(n * N_COLS, (n + 1) * N_COLS)
-                lora = products.tile([P, N_COLS], F32, tag="product")
-                nc.tensor.matmul(lora[:], lhsT=haT_sb[:, m, :], rhs=b_sb[:, cols], start=True, stop=True)
-                if m % 2 == 1 and n == 1:
-                    nc.vector.tensor_copy(out=out_sb[:, m, cols], in_=lora[:])
-                else:
-                    nc.scalar.copy(out=out_sb[:, m, cols], in_=lora[:])
+        def lora_half(m, n, on_vector=False):
+            cols = slice(n * N_COLS, (n + 1) * N_COLS)
+            lora = products.tile([P, N_COLS], F32, tag="product")
+            nc.tensor.matmul(lora[:], lhsT=haT_sb[:, m, :], rhs=b_sb[:, cols], start=True, stop=True)
+            if on_vector:
+                nc.vector.tensor_copy(out=out_sb[:, m, cols], in_=lora[:])
+            else:
+                nc.scalar.copy(out=out_sb[:, m, cols], in_=lora[:])
 
         def quantise_tokens(m):
             for g0 in range(0, PASSES, PASSES_PER_BANK):
@@ -113,7 +112,7 @@ def tile_loramlp_pb_kernel(tc, h, ha, W_down_words, W_down_scales, B_down, out):
                     in_=grouped[:, :count].rearrange("p c r t -> p (c r t)"),
                 )
 
-        def multiply_tokens(m):
+        def multiply_tokens(m, lora_of=None):
             for n in range(N_HALVES):
                 cols = slice(n * N_COLS, (n + 1) * N_COLS)
                 acc = products.tile([P, N_COLS], F32, tag="product")
@@ -133,13 +132,21 @@ def tile_loramlp_pb_kernel(tc, h, ha, W_down_words, W_down_scales, B_down, out):
                         out=out_sb[:, m, part], in0=acc[:, first : first + STORE_COLS], in1=out_sb[:, m, part]
                     )
                     nc.sync.dma_start(out=out[m * P : (m + 1) * P, part], in_=out_sb[:, m, part])
+                if lora_of is not None:
+                    lora_half(lora_of, n)
 
-        for i in range(TILES_PER_ROUND):
-            sort_words(i)
-            lora_tokens(2 * i)
-            lora_tokens(2 * i + 1)
+        sort_words(0)
+        lora_half(0, 0)
+        lora_half(0, 1)
+        lora_half(1, 0)
+        lora_half(1, 1, on_vector=True)
+        sort_words(1)
+        lora_half(2, 0)
+        lora_half(2, 1)
         for i in range(TILES_PER_ROUND):
             quantise_tokens(i)
+        lora_half(3, 0)
+        lora_half(3, 1)
 
         for m0 in range(0, TOKEN_TILES, TILES_PER_ROUND):
             upcoming = range(m0 + TILES_PER_ROUND, min(m0 + 2 * TILES_PER_ROUND, TOKEN_TILES))

@@ -64,13 +64,8 @@ def tile_loramlp_pb_kernel(tc, h, ha, W_down_words, W_down_scales, B_down, out):
                 out=w_scales[r : P : 32, :, :].bitcast(I32),
                 in_=W_down_scales[:, r : 16 : 4, :].rearrange("g q c -> q g c").bitcast(I32),
             )
-        for n in range(N_HALVES):
-            word_bytes = slice(2 * n * N_COLS, 2 * (n + 1) * N_COLS)
-            for g in range(PASSES):
-                nc.sync.dma_start(
-                    out=w_words[:, g, word_bytes].bitcast(I32),
-                    in_=W_down_words[g, :, word_bytes].bitcast(I32),
-                )
+        for g in range(PASSES):
+            nc.sync.dma_start(out=w_words[:, g, :].bitcast(I32), in_=W_down_words[g].bitcast(I32))
         load_h(2)
         load_h(3)
 
@@ -112,28 +107,40 @@ def tile_loramlp_pb_kernel(tc, h, ha, W_down_words, W_down_scales, B_down, out):
                     in_=grouped[:, :count].rearrange("p c r t -> p (c r t)"),
                 )
 
-        def multiply_tokens(m, lora_of=None):
+        def mx_pass(acc, m, n, g):
+            nc.tensor.matmul_mx(
+                out=acc[:],
+                lhsT=h_codes[:, m, g, :].bitcast(FP8X4),
+                lhsT_scale=h_scales[:, m, g, :],
+                rhs=w_words[:, g, 2 * n * N_COLS : 2 * (n + 1) * N_COLS].bitcast(FP4X4),
+                rhs_scale=w_scales[:, g, n * N_COLS : (n + 1) * N_COLS],
+                start=(g == 0),
+                stop=(g == PASSES - 1),
+            )
+
+        def add_and_store(acc, m, n):
+            for first in range(0, N_COLS, STORE_COLS):
+                part = slice(n * N_COLS + first, n * N_COLS + first + STORE_COLS)
+                nc.vector.tensor_add(
+                    out=out_sb[:, m, part], in0=acc[:, first : first + STORE_COLS], in1=out_sb[:, m, part]
+                )
+                nc.sync.dma_start(out=out[m * P : (m + 1) * P, part], in_=out_sb[:, m, part])
+
+        def multiply_tokens(m):
             for n in range(N_HALVES):
-                cols = slice(n * N_COLS, (n + 1) * N_COLS)
                 acc = products.tile([P, N_COLS], F32, tag="product")
                 for g in range(PASSES):
-                    nc.tensor.matmul_mx(
-                        out=acc[:],
-                        lhsT=h_codes[:, m, g, :].bitcast(FP8X4),
-                        lhsT_scale=h_scales[:, m, g, :],
-                        rhs=w_words[:, g, 2 * n * N_COLS : 2 * (n + 1) * N_COLS].bitcast(FP4X4),
-                        rhs_scale=w_scales[:, g, cols],
-                        start=(g == 0),
-                        stop=(g == PASSES - 1),
-                    )
-                for first in range(0, N_COLS, STORE_COLS):
-                    part = slice(n * N_COLS + first, n * N_COLS + first + STORE_COLS)
-                    nc.vector.tensor_add(
-                        out=out_sb[:, m, part], in0=acc[:, first : first + STORE_COLS], in1=out_sb[:, m, part]
-                    )
-                    nc.sync.dma_start(out=out[m * P : (m + 1) * P, part], in_=out_sb[:, m, part])
-                if lora_of is not None:
-                    lora_half(lora_of, n)
+                    mx_pass(acc, m, n, g)
+                add_and_store(acc, m, n)
+
+        def multiply_tokens_as_w_lands(m):
+            acc_0 = products.tile([P, N_COLS], F32, tag="product")
+            acc_1 = products.tile([P, N_COLS], F32, tag="product")
+            for g in range(PASSES):
+                mx_pass(acc_0, m, 0, g)
+                mx_pass(acc_1, m, 1, g)
+            add_and_store(acc_0, m, 0)
+            add_and_store(acc_1, m, 1)
 
         sort_words(0)
         lora_half(0, 0)
@@ -150,7 +157,10 @@ def tile_loramlp_pb_kernel(tc, h, ha, W_down_words, W_down_scales, B_down, out):
 
         for m0 in range(0, TOKEN_TILES, TILES_PER_ROUND):
             upcoming = range(m0 + TILES_PER_ROUND, min(m0 + 2 * TILES_PER_ROUND, TOKEN_TILES))
-            multiply_tokens(m0)
+            if m0 == 0:
+                multiply_tokens_as_w_lands(m0)
+            else:
+                multiply_tokens(m0)
             for m in upcoming:
                 sort_words(m)
             multiply_tokens(m0 + 1)

@@ -21,6 +21,7 @@ N_COLS = 512
 N_HALVES = D // N_COLS
 PASSES_PER_BANK = 2
 TILES_PER_ROUND = 2
+LAST_COLS = 128
 STORE_COLS = 256
 
 FLOPS = 2 * T * F * D + 2 * T * R * D
@@ -52,10 +53,13 @@ def tile_loramlp_pb_kernel(tc, h, ha, W_down_words, W_down_scales, B_down, out):
         make_identity(nc, ident_f32[:])
         nc.vector.tensor_copy(out=ident_bf16[:], in_=ident_f32[:])
 
-        def load_h(m):
-            nc.sync.dma_start(out=h_sb[:, m, :], in_=h[m * P : (m + 1) * P, :])
+        h_by_tile = h.rearrange("(p m) k -> p m k", p=P)
+        out_by_tile = out.rearrange("(p m) d -> p m d", p=P)
 
-        nc.sync.dma_start(out=ha_sb[:], in_=ha.rearrange("(m p) r -> p m r", p=P))
+        def load_h(m):
+            nc.sync.dma_start(out=h_sb[:, m, :], in_=h_by_tile[:, m, :])
+
+        nc.sync.dma_start(out=ha_sb[:], in_=ha.rearrange("(p m) r -> p m r", p=P))
         nc.sync.dma_start(out=b_sb[:], in_=B_down)
         load_h(0)
         load_h(1)
@@ -75,10 +79,14 @@ def tile_loramlp_pb_kernel(tc, h, ha, W_down_words, W_down_scales, B_down, out):
             nc.scalar.copy(out=haT_sb[:, m, :], in_=haT_ps[:])
 
         def sort_words(m):
-            nc.vector.tensor_copy(
-                out=h_sorted[:, m],
-                in_=h_sb[:, m, :].bitcast(F32).rearrange("r (g p u) -> r u g p", g=PASSES, u=2),
-            )
+            for g0 in range(0, PASSES, PASSES_PER_BANK):
+                count = min(PASSES_PER_BANK, PASSES - g0)
+                nc.vector.tensor_copy(
+                    out=h_sorted[:, m, :, g0 : g0 + count, :],
+                    in_=h_sb[:, m, g0 * K_PASS : (g0 + count) * K_PASS]
+                    .bitcast(F32)
+                    .rearrange("r (g p u) -> r u g p", g=count, u=2),
+                )
 
         def lora_half(m, n, on_vector=False):
             cols = slice(n * N_COLS, (n + 1) * N_COLS)
@@ -124,14 +132,36 @@ def tile_loramlp_pb_kernel(tc, h, ha, W_down_words, W_down_scales, B_down, out):
                 nc.vector.tensor_add(
                     out=out_sb[:, m, part], in0=acc[:, first : first + STORE_COLS], in1=out_sb[:, m, part]
                 )
-                nc.sync.dma_start(out=out[m * P : (m + 1) * P, part], in_=out_sb[:, m, part])
+                nc.sync.dma_start(out=out_by_tile[:, m, part], in_=out_sb[:, m, part])
 
-        def multiply_tokens(m):
+        def multiply_tokens(m, sort_between=None):
             for n in range(N_HALVES):
+                if n == 1 and sort_between is not None:
+                    sort_words(sort_between)
+                if m == TOKEN_TILES - 1 and n == N_HALVES - 1:
+                    multiply_last_half(m, n)
+                    continue
                 acc = products.tile([P, N_COLS], F32, tag="product")
                 for g in range(PASSES):
                     mx_pass(acc, m, n, g)
                 add_and_store(acc, m, n)
+
+        def multiply_last_half(m, n):
+            for first in range(n * N_COLS, (n + 1) * N_COLS, LAST_COLS):
+                acc = products.tile([P, LAST_COLS], F32, tag="product")
+                for g in range(PASSES):
+                    nc.tensor.matmul_mx(
+                        out=acc[:],
+                        lhsT=h_codes[:, m, g, :].bitcast(FP8X4),
+                        lhsT_scale=h_scales[:, m, g, :],
+                        rhs=w_words[:, g, 2 * first : 2 * (first + LAST_COLS)].bitcast(FP4X4),
+                        rhs_scale=w_scales[:, g, first : first + LAST_COLS],
+                        start=(g == 0),
+                        stop=(g == PASSES - 1),
+                    )
+                part = slice(first, first + LAST_COLS)
+                nc.vector.tensor_add(out=out_sb[:, m, part], in0=acc[:], in1=out_sb[:, m, part])
+                nc.sync.dma_start(out=out_by_tile[:, m, part], in_=out_sb[:, m, part])
 
         def multiply_tokens_as_w_lands(m):
             acc_0 = products.tile([P, N_COLS], F32, tag="product")
@@ -161,8 +191,9 @@ def tile_loramlp_pb_kernel(tc, h, ha, W_down_words, W_down_scales, B_down, out):
                 multiply_tokens_as_w_lands(m0)
             else:
                 multiply_tokens(m0)
-            for m in upcoming:
-                sort_words(m)
-            multiply_tokens(m0 + 1)
+            later = list(upcoming) + [None, None]
+            if later[0] is not None:
+                sort_words(later[0])
+            multiply_tokens(m0 + 1, sort_between=later[1])
             for m in upcoming:
                 quantise_tokens(m)

@@ -32,8 +32,7 @@ def tile_loramlp_pb_kernel(tc, h, ha, W_down_words, W_down_scales, B_down, out):
     with ExitStack() as ctx:
         keep = ctx.enter_context(tc.tile_pool(name="keep", bufs=1))
         stage = ctx.enter_context(tc.tile_pool(name="stage", bufs=6))
-        flipped = ctx.enter_context(tc.psum_pool(name="flipped", bufs=4))
-        products = ctx.enter_context(tc.psum_pool(name="products", bufs=4))
+        banks = ctx.enter_context(tc.psum_pool(name="banks", bufs=8))
         ctx.enter_context(tc.manual_schedule())
 
         h_sb = keep.tile([P, TOKEN_TILES, F], BF16)
@@ -74,7 +73,7 @@ def tile_loramlp_pb_kernel(tc, h, ha, W_down_words, W_down_scales, B_down, out):
         load_h(3)
 
         for m in range(TOKEN_TILES):
-            haT_ps = flipped.tile([P, P], BF16, tag="flipped")
+            haT_ps = banks.tile([P, P], BF16, tag="bank")
             nc.tensor.transpose(haT_ps[:], ha_sb[:, m, :], ident_bf16[:])
             nc.scalar.copy(out=haT_sb[:, m, :], in_=haT_ps[:])
 
@@ -90,7 +89,7 @@ def tile_loramlp_pb_kernel(tc, h, ha, W_down_words, W_down_scales, B_down, out):
 
         def lora_half(m, n, on_vector=False):
             cols = slice(n * N_COLS, (n + 1) * N_COLS)
-            lora = products.tile([P, N_COLS], F32, tag="product")
+            lora = banks.tile([P, N_COLS], F32, tag="bank")
             nc.tensor.matmul(lora[:], lhsT=haT_sb[:, m, :], rhs=b_sb[:, cols], start=True, stop=True)
             if on_vector:
                 nc.vector.tensor_copy(out=out_sb[:, m, cols], in_=lora[:])
@@ -100,7 +99,7 @@ def tile_loramlp_pb_kernel(tc, h, ha, W_down_words, W_down_scales, B_down, out):
         def quantise_tokens(m):
             for g0 in range(0, PASSES, PASSES_PER_BANK):
                 count = min(PASSES_PER_BANK, PASSES - g0)
-                pairsT = flipped.tile([P, PASSES_PER_BANK, 2, P], F32, tag="flipped")
+                pairsT = banks.tile([P, PASSES_PER_BANK, 2, P], F32, tag="bank")
                 for c in range(count):
                     for u in range(2):
                         nc.tensor.transpose(pairsT[:, c, u, :], h_sorted[:, m, u, g0 + c, :], ident_f32[:])
@@ -141,14 +140,14 @@ def tile_loramlp_pb_kernel(tc, h, ha, W_down_words, W_down_scales, B_down, out):
                 if m == TOKEN_TILES - 1 and n == N_HALVES - 1:
                     multiply_last_half(m, n)
                     continue
-                acc = products.tile([P, N_COLS], F32, tag="product")
+                acc = banks.tile([P, N_COLS], F32, tag="bank")
                 for g in range(PASSES):
                     mx_pass(acc, m, n, g)
                 add_and_store(acc, m, n)
 
         def multiply_last_half(m, n):
             for first in range(n * N_COLS, (n + 1) * N_COLS, LAST_COLS):
-                acc = products.tile([P, LAST_COLS], F32, tag="product")
+                acc = banks.tile([P, LAST_COLS], F32, tag="bank")
                 for g in range(PASSES):
                     nc.tensor.matmul_mx(
                         out=acc[:],
@@ -164,8 +163,8 @@ def tile_loramlp_pb_kernel(tc, h, ha, W_down_words, W_down_scales, B_down, out):
                 nc.sync.dma_start(out=out_by_tile[:, m, part], in_=out_sb[:, m, part])
 
         def multiply_tokens_as_w_lands(m):
-            acc_0 = products.tile([P, N_COLS], F32, tag="product")
-            acc_1 = products.tile([P, N_COLS], F32, tag="product")
+            acc_0 = banks.tile([P, N_COLS], F32, tag="bank")
+            acc_1 = banks.tile([P, N_COLS], F32, tag="bank")
             for g in range(PASSES):
                 mx_pass(acc_0, m, 0, g)
                 mx_pass(acc_1, m, 1, g)

from contextlib import ExitStack

import concourse.mybir as mybir
from concourse.masks import make_identity

F32 = mybir.dt.float32
BF16 = mybir.dt.bfloat16
I32 = mybir.dt.int32
U32 = mybir.dt.uint32
U8 = mybir.dt.uint8
FP8X4 = mybir.dt.float8_e4m3fn_x4
FP4X4 = mybir.dt.float4_e2m1fn_x4

T, D, F, R = 512, 1024, 2560, 128
P = 128
PACK = 4
K_PASS = P * PACK
PASSES = F // K_PASS
TOKEN_TILES = T // P
N_COLS = 512
N_HALVES = D // N_COLS
PASSES_PER_BANK = 2
TILES_PER_ROUND = 2
LAST_COLS = 128
STORE_COLS = 256

FLOPS = 2 * T * F * D + 2 * T * R * D


def tile_loramlp_pb_kernel(tc, h, ha, W_down_words, W_down_scales, B_down, out):
    nc = tc.nc
    with ExitStack() as ctx:
        keep = ctx.enter_context(tc.tile_pool(name="keep", bufs=1))
        stage = ctx.enter_context(tc.tile_pool(name="stage", bufs=6))
        banks = ctx.enter_context(tc.psum_pool(name="banks", bufs=8))
        ctx.enter_context(tc.manual_schedule())

        h_sb = keep.tile([P, TOKEN_TILES, F], BF16)
        h_sorted = keep.tile([P, TOKEN_TILES, 2, PASSES, P], F32)
        ha_sb = keep.tile([P, TOKEN_TILES, R], BF16)
        haT_sb = keep.tile([P, TOKEN_TILES, P], BF16)
        b_sb = keep.tile([P, D], BF16)
        w_words = keep.tile([P, PASSES, 2 * D], U8, align_bytes=64)
        w_scales = keep.tile([P, PASSES, D], U8, align_bytes=64)
        h_codes = keep.tile([P, TOKEN_TILES, PASSES, P], U32, align_bytes=64)
        h_scales = keep.tile([P, TOKEN_TILES, PASSES, P], U8, align_bytes=64)
        out_sb = keep.tile([P, TOKEN_TILES, D], F32)
        ident_f32 = keep.tile([P, P], F32)
        ident_bf16 = keep.tile([P, P], BF16)

        nc.vector.memset(w_scales[:].bitcast(I32), 0)
        make_identity(nc, ident_f32[:])
        nc.vector.tensor_copy(out=ident_bf16[:], in_=ident_f32[:])

        h_by_tile = h.rearrange("(p m) k -> p m k", p=P)
        out_by_tile = out.rearrange("(p m) d -> p m d", p=P)

        def load_h(m):
            nc.sync.dma_start(out=h_sb[:, m, :], in_=h_by_tile[:, m, :])

        nc.sync.dma_start(out=ha_sb[:], in_=ha.rearrange("(p m) r -> p m r", p=P))
        nc.sync.dma_start(out=b_sb[:], in_=B_down)
        load_h(0)
        load_h(1)
        for r in range(4):
            nc.sync.dma_start(
                out=w_scales[r : P : 32, :, :].bitcast(I32),
                in_=W_down_scales[:, r : 16 : 4, :].rearrange("g q c -> q g c").bitcast(I32),
            )
        for g in range(PASSES):
            nc.sync.dma_start(out=w_words[:, g, :].bitcast(I32), in_=W_down_words[g].bitcast(I32))
        load_h(2)
        load_h(3)

        for m in range(TOKEN_TILES):
            haT_ps = banks.tile([P, P], BF16, tag="bank")
            nc.tensor.transpose(haT_ps[:], ha_sb[:, m, :], ident_bf16[:])
            nc.scalar.copy(out=haT_sb[:, m, :], in_=haT_ps[:])

        def sort_words(m):
            for g0 in range(0, PASSES, PASSES_PER_BANK):
                count = min(PASSES_PER_BANK, PASSES - g0)
                nc.vector.tensor_copy(
                    out=h_sorted[:, m, :, g0 : g0 + count, :],
                    in_=h_sb[:, m, g0 * K_PASS : (g0 + count) * K_PASS]
                    .bitcast(F32)
                    .rearrange("r (g p u) -> r u g p", g=count, u=2),
                )

        def lora_half(m, n, on_vector=False):
            cols = slice(n * N_COLS, (n + 1) * N_COLS)
            lora = banks.tile([P, N_COLS], F32, tag="bank")
            nc.tensor.matmul(lora[:], lhsT=haT_sb[:, m, :], rhs=b_sb[:, cols], start=True, stop=True)
            if on_vector:
                nc.vector.tensor_copy(out=out_sb[:, m, cols], in_=lora[:])
            else:
                nc.scalar.copy(out=out_sb[:, m, cols], in_=lora[:])

        def quantise_tokens(m):
            for g0 in range(0, PASSES, PASSES_PER_BANK):
                count = min(PASSES_PER_BANK, PASSES - g0)
                pairsT = banks.tile([P, PASSES_PER_BANK, 2, P], F32, tag="bank")
                for c in range(count):
                    for u in range(2):
                        nc.tensor.transpose(pairsT[:, c, u, :], h_sorted[:, m, u, g0 + c, :], ident_f32[:])
                grouped = stage.tile([P, PASSES_PER_BANK, P, PACK], BF16, align_bytes=64)
                nc.scalar.copy(
                    out=grouped[:, :count].bitcast(F32),
                    in_=pairsT[:, :count].rearrange("p c u r -> p c r u"),
                )
                nc.vector.quantize_mx(
                    out=h_codes[:, m, g0 : g0 + count, :].rearrange("p c r -> p (c r)").bitcast(FP8X4),
                    scales=h_scales[:, m, g0 : g0 + count, :].rearrange("p c r -> p (c r)"),
                    in_=grouped[:, :count].rearrange("p c r t -> p (c r t)"),
                )

        def mx_pass(acc, m, n, g):
            nc.tensor.matmul_mx(
                out=acc[:],
                lhsT=h_codes[:, m, g, :].bitcast(FP8X4),
                lhsT_scale=h_scales[:, m, g, :],
                rhs=w_words[:, g, 2 * n * N_COLS : 2 * (n + 1) * N_COLS].bitcast(FP4X4),
                rhs_scale=w_scales[:, g, n * N_COLS : (n + 1) * N_COLS],
                start=(g == 0),
                stop=(g == PASSES - 1),
            )

        def add_and_store(acc, m, n):
            for first in range(0, N_COLS, STORE_COLS):
                part = slice(n * N_COLS + first, n * N_COLS + first + STORE_COLS)
                nc.vector.tensor_add(
                    out=out_sb[:, m, part], in0=acc[:, first : first + STORE_COLS], in1=out_sb[:, m, part]
                )
                nc.sync.dma_start(out=out_by_tile[:, m, part], in_=out_sb[:, m, part])

        def multiply_tokens(m, sort_between=None):
            for n in range(N_HALVES):
                if n == 1 and sort_between is not None:
                    sort_words(sort_between)
                if m == TOKEN_TILES - 1 and n == N_HALVES - 1:
                    multiply_last_half(m, n)
                    continue
                acc = banks.tile([P, N_COLS], F32, tag="bank")
                for g in range(PASSES):
                    mx_pass(acc, m, n, g)
                add_and_store(acc, m, n)

        def multiply_last_half(m, n):
            for first in range(n * N_COLS, (n + 1) * N_COLS, LAST_COLS):
                acc = banks.tile([P, LAST_COLS], F32, tag="bank")
                for g in range(PASSES):
                    nc.tensor.matmul_mx(
                        out=acc[:],
                        lhsT=h_codes[:, m, g, :].bitcast(FP8X4),
                        lhsT_scale=h_scales[:, m, g, :],
                        rhs=w_words[:, g, 2 * first : 2 * (first + LAST_COLS)].bitcast(FP4X4),
                        rhs_scale=w_scales[:, g, first : first + LAST_COLS],
                        start=(g == 0),
                        stop=(g == PASSES - 1),
                    )
                part = slice(first, first + LAST_COLS)
                nc.vector.tensor_add(out=out_sb[:, m, part], in0=acc[:], in1=out_sb[:, m, part])
                nc.sync.dma_start(out=out_by_tile[:, m, part], in_=out_sb[:, m, part])

        def multiply_tokens_as_w_lands(m):
            acc_0 = banks.tile([P, N_COLS], F32, tag="bank")
            acc_1 = banks.tile([P, N_COLS], F32, tag="bank")
            for g in range(PASSES):
                mx_pass(acc_0, m, 0, g)
                mx_pass(acc_1, m, 1, g)
            add_and_store(acc_0, m, 0)
            add_and_store(acc_1, m, 1)

        sort_words(0)
        lora_half(0, 0)
        lora_half(0, 1)
        lora_half(1, 0)
        lora_half(1, 1, on_vector=True)
        sort_words(1)
        lora_half(2, 0)
        lora_half(2, 1)
        for i in range(TILES_PER_ROUND):
            quantise_tokens(i)
        lora_half(3, 0)
        lora_half(3, 1)

        for m0 in range(0, TOKEN_TILES, TILES_PER_ROUND):
            upcoming = range(m0 + TILES_PER_ROUND, min(m0 + 2 * TILES_PER_ROUND, TOKEN_TILES))
            if m0 == 0:
                multiply_tokens_as_w_lands(m0)
            else:
                multiply_tokens(m0)
            later = list(upcoming) + [None, None]
            if later[0] is not None:
                sort_words(later[0])
            multiply_tokens(m0 + 1, sort_between=later[1])
            for m in upcoming:
                quantise_tokens(m)
